import numpy as np
import ml_dtypes


def mxq(x, axis, fmt="e4m3"):
    dtype, down = {"e4m3": (ml_dtypes.float8_e4m3fn, 7), "e5m2": (ml_dtypes.float8_e5m2, 14)}[fmt]
    v = np.moveaxis(np.asarray(x, np.float32).astype(ml_dtypes.bfloat16).astype(np.float64), axis, -1)
    blocks = v.reshape(v.shape[:-1] + (-1, 32))
    amax = np.abs(blocks).max(-1, keepdims=True)
    byte = np.maximum(np.where(amax > 0, np.frexp(amax)[1] - 1 + 127, 0) - down, 1)
    scale = np.exp2(byte - 127.0)
    codes = (blocks / scale).astype(np.float32).astype(dtype).astype(np.float64)
    return np.moveaxis((codes * scale).reshape(v.shape), -1, axis)


WIDE = False


def mx_kscale(k):
    if not WIDE:
        return np.ones(k)
    levels = np.array([10, -10, 5, -5, 0])
    a = np.random.permutation(np.resize(levels, k // 512 * 4)).reshape(k // 512, 4)
    idx = np.arange(k)
    return np.exp2(a[idx // 512, idx % 128 // 32])


BF16 = ml_dtypes.bfloat16


def bf(x):
    return np.asarray(x, np.float32).astype(BF16)


def f64(x):
    return np.asarray(x).astype(np.float64)


N, WI, H, DH, WO = 128, 8192, 4, 512, 1024
F = WO // H
EPSILON = 1e-06
XS = 0.002


def setup_inputs():
    s = mx_kscale(WI)
    return {"x": bf(np.random.standard_normal((N, WI)) * XS * s),
            "norm_bias": bf(np.random.standard_normal((N, H, DH))),
            "w_lin": bf(np.random.standard_normal((WI, H * DH)) / np.sqrt(WI) / s[:, None]),
            "kernel": bf(np.random.standard_normal((H, DH, F)) / np.sqrt(DH))}


def reference(x, norm_bias, w_lin, kernel):
    xx = mxq(f64(x), 1, "e4m3") @ mxq(f64(w_lin), 0, "e4m3")
    xx = xx.reshape(N, H, DH)
    xx = xx / np.sqrt(np.mean(np.square(xx), axis=-1, keepdims=True) + EPSILON)
    xx = (xx + f64(norm_bias).reshape(xx.shape)) / np.sqrt(2.0)
    xh = xx.transpose(1, 0, 2)
    y = mxq(xh, 2, "e4m3") @ mxq(f64(kernel), 1, "e4m3")
    return y.transpose(1, 0, 2).reshape(N, H * F)

@@ -1,0 +1,231 @@
+from contextlib import ExitStack
+import math
+
+import concourse.masks as masks
+import concourse.mybir as mybir
+
+BF16 = mybir.dt.bfloat16
+F32 = mybir.dt.float32
+U32 = mybir.dt.uint32
+U8 = mybir.dt.uint8
+FP8X4 = mybir.dt.float8_e4m3fn_x4
+ACT = mybir.ActivationFunctionType
+ALU = mybir.AluOpType
+
+P = 128
+PACK = 4
+K_PASS = P * PACK
+TOKENS = 128
+WI = 8192
+HEADS = 4
+DH = 512
+F = 256
+WIDTH = HEADS * DH
+PASSES = WI // K_PASS
+EPSILON = 1e-6
+
+HALF = WIDTH // 2
+QUANT_IN = HALF * PACK
+RUN = 4
+RAW_BUFS = 5
+GROUPED_BUFS = 6
+
+FLOPS = 2 * TOKENS * WI * WIDTH + 2 * TOKENS * DH * F * HEADS
+
+
+def regroup(copy, grouped, rows):
+    copy(
+        out=grouped.rearrange("p (c i j) -> p c j i", i=RUN, j=PACK),
+        in_=rows.rearrange("p j (c i) -> p c j i", i=RUN),
+    )
+
+
+def tile_grouplinearblock_pa_k_kernel(tc, x, norm_bias, w_lin, kernel, out):
+    nc = tc.nc
+    with ExitStack() as ctx:
+        keep = ctx.enter_context(tc.tile_pool(name="keep", bufs=1))
+        raw_pool = ctx.enter_context(tc.tile_pool(name="raw", bufs=RAW_BUFS))
+        grouped_pool = ctx.enter_context(tc.tile_pool(name="grouped", bufs=GROUPED_BUFS))
+        operand_pool = ctx.enter_context(tc.tile_pool(name="operand", bufs=GROUPED_BUFS))
+        acc_pool = ctx.enter_context(tc.psum_pool(name="acc", bufs=1))
+        work = ctx.enter_context(tc.psum_pool(name="work", bufs=4))
+        ctx.enter_context(tc.manual_schedule())
+
+        def quantise(grouped, codes, scales):
+            nc.vector.quantize_mx(out=codes.bitcast(FP8X4), scales=scales, in_=grouped)
+
+        ident_f32 = keep.tile([P, P], F32)
+        masks.make_identity(nc, ident_f32[:])
+        ident_bf16 = keep.tile([P, P], BF16)
+        masks.make_identity(nc, ident_bf16[:])
+        two_eps = keep.tile([P, 1], F32)
+        nc.vector.memset(two_eps[:], 2.0 * EPSILON)
+        table_warm = keep.tile([P, 1], F32)
+        nc.scalar.activation(out=table_warm[:], in_=two_eps[:], func=ACT.Sqrt)
+
+        x_rows = raw_pool.tile([P, WI], BF16, tag="raw")
+        x_piece = WI // 4
+        for q in range(4):
+            cols = slice(q * x_piece, (q + 1) * x_piece)
+            nc.sync.dma_start(out=x_rows[:, cols], in_=x[:, cols])
+        k_rows = raw_pool.tile([P, HEADS, PACK, F], BF16, tag="raw")
+        nc.sync.dma_start(out=k_rows[:], in_=kernel.rearrange("h (p j) f -> p h j f", j=PACK))
+        bias_rows = keep.tile([P, HEADS, DH], BF16)
+        nc.sync.dma_start(out=bias_rows[:], in_=norm_bias)
+
+        x_words = x_rows[:].bitcast(F32).rearrange("m (c p u) -> m c u p", p=P, u=2)
+        x_grouped = [
+            grouped_pool.tile([P, QUANT_IN], BF16, tag="grouped", name="x_grouped%d" % g, align_bytes=64)
+            for g in range(2)
+        ]
+        x_codes = keep.tile([P, PASSES * TOKENS], U32, align_bytes=64)
+        x_scales = keep.tile([P, PASSES * TOKENS], U8, align_bytes=64)
+        for b in range(PASSES // 2):
+            turned = work.tile([P, 2, 2, TOKENS], F32, tag="work")
+            for cc in range(2):
+                for u in range(2):
+                    nc.tensor.transpose(
+                        out=turned[:, cc, u, :], in_=x_words[:, 2 * b + cc, u, :], identity=ident_f32[:]
+                    )
+            words = x_grouped[b // 4][:].bitcast(F32)[:, (b % 4) * 512 : (b % 4 + 1) * 512]
+            copy = nc.scalar.copy if b % 2 == 0 else nc.vector.tensor_copy
+            copy(
+                out=words.rearrange("p (c r u) -> p c r u", c=2, u=2),
+                in_=turned[:].rearrange("p c u r -> p c r u"),
+            )
+        for g in range(2):
+            cols = slice(g * HALF, (g + 1) * HALF)
+            quantise(x_grouped[g][:], x_codes[:, cols], x_scales[:, cols])
+
+        k_grouped = grouped_pool.tile([P, QUANT_IN], BF16, tag="grouped", align_bytes=64)
+        k_codes = keep.tile([P, HEADS * F], U32, align_bytes=64)
+        k_scales = keep.tile([P, HEADS * F], U8, align_bytes=64)
+        for h in range(HEADS):
+            copy = nc.scalar.copy if h % 2 == 0 else nc.vector.tensor_copy
+            regroup(copy, k_grouped[:, h * F * PACK : (h + 1) * F * PACK], k_rows[:, h])
+        quantise(k_grouped[:], k_codes[:], k_scales[:])
+
+        bias_scaled = keep.tile([P, HEADS, PACK, P], F32)
+        nc.scalar.mul(
+            out=bias_scaled[:],
+            in_=bias_rows[:].rearrange("m h (p j) -> m h j p", j=PACK),
+            mul=1.0 / math.sqrt(2.0),
+        )
+
+        acc = [acc_pool.tile([P, DH], F32, name="acc%d" % h) for h in range(HEADS)]
+
+        def quantise_and_project(c, heads, grouped):
+            codes = operand_pool.tile([P, HALF], U32, tag="codes", align_bytes=64)
+            scales = operand_pool.tile([P, HALF], U8, tag="scales", align_bytes=64)
+            quantise(grouped[:], codes[:], scales[:])
+            tokens = slice(c * TOKENS, (c + 1) * TOKENS)
+            for n, h in enumerate(heads):
+                cols = slice(n * DH, (n + 1) * DH)
+                nc.tensor.matmul_mx(
+                    out=acc[h][:],
+                    lhsT=x_codes[:, tokens].bitcast(FP8X4),
+                    lhsT_scale=x_scales[:, tokens],
+                    rhs=codes[:, cols].bitcast(FP8X4),
+                    rhs_scale=scales[:, cols],
+                    start=(c == 0),
+                    stop=(c == PASSES - 1),
+                )
+
+        waiting = None
+        for c in range(PASSES):
+            rows = raw_pool.tile([P, PACK, WIDTH], BF16, tag="raw")
+            nc.sync.dma_start(
+                out=rows[:], in_=w_lin[c * K_PASS : (c + 1) * K_PASS, :].rearrange("(p j) w -> p j w", j=PACK)
+            )
+            by_scalar = grouped_pool.tile([P, QUANT_IN], BF16, tag="grouped", align_bytes=64)
+            regroup(nc.scalar.copy, by_scalar[:], rows[:, :, 0:HALF])
+            by_vector = grouped_pool.tile([P, QUANT_IN], BF16, tag="grouped", align_bytes=64)
+            regroup(nc.vector.tensor_copy, by_vector[:], rows[:, :, HALF:WIDTH])
+            if c > 0:
+                quantise_and_project(c - 1, (0, 1), waiting)
+            quantise_and_project(c, (2, 3), by_vector)
+            waiting = by_scalar
+        quantise_and_project(PASSES - 1, (0, 1), waiting)
+
+        squares = keep.tile([P, HEADS, DH], BF16)
+        sum_sq = keep.tile([P, HEADS], F32)
+        root = keep.tile([P, HEADS], F32)
+        gain = keep.tile([P, HEADS], F32)
+        u_grouped = keep.tile([P, HEADS * TOKENS * PACK], BF16, align_bytes=64)
+        u_codes = keep.tile([P, HEADS * TOKENS], U32, align_bytes=64)
+        u_scales = keep.tile([P, HEADS * TOKENS], U8, align_bytes=64)
+        out_rows = keep.tile([P, HEADS * F], F32)
+
+        def square_sums(pair):
+            for h in pair:
+                nc.scalar.activation(
+                    out=squares[:, h, :], in_=acc[h][:], func=ACT.Square, accum_out=sum_sq[:, h : h + 1]
+                )
+            both = slice(pair[0], pair[0] + 2)
+            nc.scalar.activation(
+                out=root[:, both], in_=sum_sq[:, both], func=ACT.Sqrt, scale=2.0 / DH, bias=two_eps[:]
+            )
+
+        def gains(pair):
+            both = slice(pair[0], pair[0] + 2)
+            nc.vector.reciprocal(out=gain[:, both], in_=root[:, both])
+
+        turned_u = {}
+
+        def blend(h):
+            u = keep.tile([P, PACK, P], BF16, name="u%d" % h)
+            nc.vector.scalar_tensor_tensor(
+                out=u[:],
+                in0=acc[h][:].rearrange("m (p j) -> m j p", j=PACK),
+                scalar=gain[:, h : h + 1],
+                in1=bias_scaled[:, h],
+                op0=ALU.mult,
+                op1=ALU.add,
+            )
+            turned_u[h] = work.tile([P, PACK, TOKENS], BF16, tag="work", name="turned_u%d" % h)
+            for j in range(PACK):
+                nc.tensor.transpose(out=turned_u[h][:, j, :], in_=u[:, j, :], identity=ident_bf16[:])
+
+        def gather(h):
+            nc.scalar.copy(
+                out=u_grouped[:, h * K_PASS : (h + 1) * K_PASS].rearrange("p (r j) -> p r j", j=PACK),
+                in_=turned_u[h][:].rearrange("p j r -> p r j"),
+            )
+
+        def second_product(pair):
+            lo = pair[0]
+            quantise(
+                u_grouped[:, lo * K_PASS : (lo + 2) * K_PASS],
+                u_codes[:, lo * TOKENS : (lo + 2) * TOKENS],
+                u_scales[:, lo * TOKENS : (lo + 2) * TOKENS],
+            )
+            for h in pair:
+                y = work.tile([P, F], F32, tag="work")
+                nc.tensor.matmul_mx(
+                    out=y[:],
+                    lhsT=u_codes[:, h * TOKENS : (h + 1) * TOKENS].bitcast(FP8X4),
+                    lhsT_scale=u_scales[:, h * TOKENS : (h + 1) * TOKENS],
+                    rhs=k_codes[:, h * F : (h + 1) * F].bitcast(FP8X4),
+                    rhs_scale=k_scales[:, h * F : (h + 1) * F],
+                    start=True,
+                    stop=True,
+                )
+                copy = nc.scalar.copy if h % 2 == 0 else nc.vector.tensor_copy
+                copy(out=out_rows[:, h * F : (h + 1) * F], in_=y[:])
+            nc.sync.dma_start(out=out[:, lo * F : (lo + 2) * F], in_=out_rows[:, lo * F : (lo + 2) * F])
+
+        first, last = (2, 3), (0, 1)
+        square_sums(first)
+        gains(first)
+        square_sums(last)
+        blend(2)
+        blend(3)
+        gains(last)
+        gather(2)
+        gather(3)
+        blend(0)
+        blend(1)
+        gather(0)
+        gather(1)
+        second_product(first)
+        second_product(last)

@@ -56,22 +56,16 @@ def tile_grouplinearblock_pa_k_kernel(tc, x, norm_bias, w_lin, kernel, out):
 
         ident_f32 = keep.tile([P, P], F32)
         masks.make_identity(nc, ident_f32[:])
-        ident_bf16 = keep.tile([P, P], BF16)
-        masks.make_identity(nc, ident_bf16[:])
-        two_eps = keep.tile([P, 1], F32)
-        nc.vector.memset(two_eps[:], 2.0 * EPSILON)
+        eps = keep.tile([P, 1], F32)
+        nc.vector.memset(eps[:], EPSILON)
         table_warm = keep.tile([P, 1], F32)
-        nc.scalar.activation(out=table_warm[:], in_=two_eps[:], func=ACT.Sqrt)
+        nc.scalar.activation(out=table_warm[:], in_=eps[:], func=ACT.Sqrt)
 
         x_rows = raw_pool.tile([P, WI], BF16, tag="raw")
         x_piece = WI // 4
         for q in range(4):
             cols = slice(q * x_piece, (q + 1) * x_piece)
             nc.sync.dma_start(out=x_rows[:, cols], in_=x[:, cols])
-        k_rows = raw_pool.tile([P, HEADS, PACK, F], BF16, tag="raw")
-        nc.sync.dma_start(out=k_rows[:], in_=kernel.rearrange("h (p j) f -> p h j f", j=PACK))
-        bias_rows = keep.tile([P, HEADS, DH], BF16)
-        nc.sync.dma_start(out=bias_rows[:], in_=norm_bias)
 
         x_words = x_rows[:].bitcast(F32).rearrange("m (c p u) -> m c u p", p=P, u=2)
         x_grouped = [
@@ -96,21 +90,6 @@ def tile_grouplinearblock_pa_k_kernel(tc, x, norm_bias, w_lin, kernel, out):
         for g in range(2):
             cols = slice(g * HALF, (g + 1) * HALF)
             quantise(x_grouped[g][:], x_codes[:, cols], x_scales[:, cols])
-
-        k_grouped = grouped_pool.tile([P, QUANT_IN], BF16, tag="grouped", align_bytes=64)
-        k_codes = keep.tile([P, HEADS * F], U32, align_bytes=64)
-        k_scales = keep.tile([P, HEADS * F], U8, align_bytes=64)
-        for h in range(HEADS):
-            copy = nc.scalar.copy if h % 2 == 0 else nc.vector.tensor_copy
-            regroup(copy, k_grouped[:, h * F * PACK : (h + 1) * F * PACK], k_rows[:, h])
-        quantise(k_grouped[:], k_codes[:], k_scales[:])
-
-        bias_scaled = keep.tile([P, HEADS, PACK, P], F32)
-        nc.scalar.mul(
-            out=bias_scaled[:],
-            in_=bias_rows[:].rearrange("m h (p j) -> m h j p", j=PACK),
-            mul=1.0 / math.sqrt(2.0),
-        )
 
         acc = [acc_pool.tile([P, DH], F32, name="acc%d" % h) for h in range(HEADS)]
 
@@ -145,7 +124,19 @@ def tile_grouplinearblock_pa_k_kernel(tc, x, norm_bias, w_lin, kernel, out):
                 quantise_and_project(c - 1, (0, 1), waiting)
             quantise_and_project(c, (2, 3), by_vector)
             waiting = by_scalar
+
+        k_rows = keep.tile([P, HEADS, PACK, F], BF16)
+        nc.sync.dma_start(out=k_rows[:], in_=kernel.rearrange("h (p j) f -> p h j f", j=PACK))
+        bias_rows = keep.tile([P, HEADS, DH], BF16)
+        nc.sync.dma_start(out=bias_rows[:], in_=norm_bias)
+        k_grouped = keep.tile([P, QUANT_IN], BF16, align_bytes=64)
+        k_codes = keep.tile([P, HEADS * F], U32, align_bytes=64)
+        k_scales = keep.tile([P, HEADS * F], U8, align_bytes=64)
+        for h in range(HEADS):
+            regroup(nc.scalar.copy, k_grouped[:, h * F * PACK : (h + 1) * F * PACK], k_rows[:, h])
+
         quantise_and_project(PASSES - 1, (0, 1), waiting)
+        quantise(k_grouped[:], k_codes[:], k_scales[:])
 
         squares = keep.tile([P, HEADS, DH], BF16)
         sum_sq = keep.tile([P, HEADS], F32)
@@ -163,7 +154,7 @@ def tile_grouplinearblock_pa_k_kernel(tc, x, norm_bias, w_lin, kernel, out):
                 )
             both = slice(pair[0], pair[0] + 2)
             nc.scalar.activation(
-                out=root[:, both], in_=sum_sq[:, both], func=ACT.Sqrt, scale=2.0 / DH, bias=two_eps[:]
+                out=root[:, both], in_=sum_sq[:, both], func=ACT.Sqrt, scale=1.0 / DH, bias=eps[:]
             )
 
         def gains(pair):
@@ -173,23 +164,24 @@ def tile_grouplinearblock_pa_k_kernel(tc, x, norm_bias, w_lin, kernel, out):
         turned_u = {}
 
         def blend(h):
-            u = keep.tile([P, PACK, P], BF16, name="u%d" % h)
+            mixed = keep.tile([P, PACK, P], F32, name="mixed%d" % h)
             nc.vector.scalar_tensor_tensor(
-                out=u[:],
+                out=mixed[:],
                 in0=acc[h][:].rearrange("m (p j) -> m j p", j=PACK),
                 scalar=gain[:, h : h + 1],
-                in1=bias_scaled[:, h],
+                in1=bias_rows[:, h, :].rearrange("m (p j) -> m j p", j=PACK),
                 op0=ALU.mult,
                 op1=ALU.add,
             )
-            turned_u[h] = work.tile([P, PACK, TOKENS], BF16, tag="work", name="turned_u%d" % h)
+            turned_u[h] = work.tile([P, PACK, TOKENS], F32, tag="work", name="turned_u%d" % h)
             for j in range(PACK):
-                nc.tensor.transpose(out=turned_u[h][:, j, :], in_=u[:, j, :], identity=ident_bf16[:])
+                nc.tensor.transpose(out=turned_u[h][:, j, :], in_=mixed[:, j, :], identity=ident_f32[:])
 
         def gather(h):
-            nc.scalar.copy(
+            nc.scalar.mul(
                 out=u_grouped[:, h * K_PASS : (h + 1) * K_PASS].rearrange("p (r j) -> p r j", j=PACK),
                 in_=turned_u[h][:].rearrange("p j r -> p r j"),
+                mul=1.0 / math.sqrt(2.0),
             )
 
         def second_product(pair):

@@ -29,6 +29,7 @@ QUANT_IN = HALF * PACK
 RUN = 4
 RAW_BUFS = 5
 GROUPED_BUFS = 6
+FINISH_ORDER = [0, 2, 1, 3]
 
 FLOPS = 2 * TOKENS * WI * WIDTH + 2 * TOKENS * DH * F * HEADS
 
@@ -54,8 +55,8 @@ def tile_grouplinearblock_pa_k_kernel(tc, x, norm_bias, w_lin, kernel, out):
         def quantise(grouped, codes, scales):
             nc.vector.quantize_mx(out=codes.bitcast(FP8X4), scales=scales, in_=grouped)
 
-        ident_f32 = keep.tile([P, P], F32)
-        masks.make_identity(nc, ident_f32[:])
+        ident = keep.tile([P, P], F32)
+        masks.make_identity(nc, ident[:])
         eps = keep.tile([P, 1], F32)
         nc.vector.memset(eps[:], EPSILON)
         table_warm = keep.tile([P, 1], F32)
@@ -66,6 +67,8 @@ def tile_grouplinearblock_pa_k_kernel(tc, x, norm_bias, w_lin, kernel, out):
         for q in range(4):
             cols = slice(q * x_piece, (q + 1) * x_piece)
             nc.sync.dma_start(out=x_rows[:, cols], in_=x[:, cols])
+        k_rows = raw_pool.tile([P, HEADS, PACK, F], BF16, tag="raw")
+        nc.sync.dma_start(out=k_rows[:], in_=kernel.rearrange("h (p j) f -> p h j f", j=PACK))
 
         x_words = x_rows[:].bitcast(F32).rearrange("m (c p u) -> m c u p", p=P, u=2)
         x_grouped = [
@@ -79,7 +82,7 @@ def tile_grouplinearblock_pa_k_kernel(tc, x, norm_bias, w_lin, kernel, out):
             for cc in range(2):
                 for u in range(2):
                     nc.tensor.transpose(
-                        out=turned[:, cc, u, :], in_=x_words[:, 2 * b + cc, u, :], identity=ident_f32[:]
+                        out=turned[:, cc, u, :], in_=x_words[:, 2 * b + cc, u, :], identity=ident[:]
                     )
             words = x_grouped[b // 4][:].bitcast(F32)[:, (b % 4) * 512 : (b % 4 + 1) * 512]
             copy = nc.scalar.copy if b % 2 == 0 else nc.vector.tensor_copy
@@ -91,12 +94,21 @@ def tile_grouplinearblock_pa_k_kernel(tc, x, norm_bias, w_lin, kernel, out):
             cols = slice(g * HALF, (g + 1) * HALF)
             quantise(x_grouped[g][:], x_codes[:, cols], x_scales[:, cols])
 
+        k_grouped = grouped_pool.tile([P, QUANT_IN], BF16, tag="grouped", align_bytes=64)
+        k_codes = keep.tile([P, HEADS * F], U32, align_bytes=64)
+        k_scales = keep.tile([P, HEADS * F], U8, align_bytes=64)
+        for h in range(HEADS):
+            copy = nc.scalar.copy if h % 2 == 0 else nc.vector.tensor_copy
+            regroup(copy, k_grouped[:, h * F * PACK : (h + 1) * F * PACK], k_rows[:, h])
+        quantise(k_grouped[:], k_codes[:], k_scales[:])
+
         acc = [acc_pool.tile([P, DH], F32, name="acc%d" % h) for h in range(HEADS)]
 
         def quantise_and_project(c, heads, grouped):
+            width = len(heads) * DH
             codes = operand_pool.tile([P, HALF], U32, tag="codes", align_bytes=64)
             scales = operand_pool.tile([P, HALF], U8, tag="scales", align_bytes=64)
-            quantise(grouped[:], codes[:], scales[:])
+            quantise(grouped, codes[:, 0:width], scales[:, 0:width])
             tokens = slice(c * TOKENS, (c + 1) * TOKENS)
             for n, h in enumerate(heads):
                 cols = slice(n * DH, (n + 1) * DH)
@@ -110,33 +122,38 @@ def tile_grouplinearblock_pa_k_kernel(tc, x, norm_bias, w_lin, kernel, out):
                     stop=(c == PASSES - 1),
                 )
 
+        def pass_rows(c):
+            return w_lin[c * K_PASS : (c + 1) * K_PASS, :].rearrange("(p j) w -> p j w", j=PACK)
+
         waiting = None
-        for c in range(PASSES):
+        for c in range(PASSES - 1):
             rows = raw_pool.tile([P, PACK, WIDTH], BF16, tag="raw")
-            nc.sync.dma_start(
-                out=rows[:], in_=w_lin[c * K_PASS : (c + 1) * K_PASS, :].rearrange("(p j) w -> p j w", j=PACK)
-            )
+            nc.sync.dma_start(out=rows[:], in_=pass_rows(c))
             by_scalar = grouped_pool.tile([P, QUANT_IN], BF16, tag="grouped", align_bytes=64)
             regroup(nc.scalar.copy, by_scalar[:], rows[:, :, 0:HALF])
             by_vector = grouped_pool.tile([P, QUANT_IN], BF16, tag="grouped", align_bytes=64)
             regroup(nc.vector.tensor_copy, by_vector[:], rows[:, :, HALF:WIDTH])
             if c > 0:
-                quantise_and_project(c - 1, (0, 1), waiting)
-            quantise_and_project(c, (2, 3), by_vector)
+                quantise_and_project(c - 1, (0, 1), waiting[:])
+            quantise_and_project(c, (2, 3), by_vector[:])
             waiting = by_scalar
 
-        k_rows = keep.tile([P, HEADS, PACK, F], BF16)
-        nc.sync.dma_start(out=k_rows[:], in_=kernel.rearrange("h (p j) f -> p h j f", j=PACK))
+        c = PASSES - 1
+        rows = raw_pool.tile([P, PACK, WIDTH], BF16, tag="raw")
+        for h in FINISH_ORDER:
+            cols = slice(h * DH, (h + 1) * DH)
+            nc.sync.dma_start(out=rows[:, :, cols], in_=pass_rows(c)[:, :, cols])
         bias_rows = keep.tile([P, HEADS, DH], BF16)
         nc.sync.dma_start(out=bias_rows[:], in_=norm_bias)
-        k_grouped = keep.tile([P, QUANT_IN], BF16, align_bytes=64)
-        k_codes = keep.tile([P, HEADS * F], U32, align_bytes=64)
-        k_scales = keep.tile([P, HEADS * F], U8, align_bytes=64)
-        for h in range(HEADS):
-            regroup(nc.scalar.copy, k_grouped[:, h * F * PACK : (h + 1) * F * PACK], k_rows[:, h])
-
-        quantise_and_project(PASSES - 1, (0, 1), waiting)
-        quantise(k_grouped[:], k_codes[:], k_scales[:])
+        quantise_and_project(c - 1, (0, 1), waiting[:])
+        by_scalar = grouped_pool.tile([P, QUANT_IN], BF16, tag="grouped", align_bytes=64)
+        by_vector = grouped_pool.tile([P, QUANT_IN], BF16, tag="grouped", align_bytes=64)
+        for n in range(2):
+            part = slice(n * DH * PACK, (n + 1) * DH * PACK)
+            regroup(nc.scalar.copy, by_scalar[:, part], rows[:, :, n * DH : (n + 1) * DH])
+            regroup(nc.vector.tensor_copy, by_vector[:, part], rows[:, :, HALF + n * DH : HALF + (n + 1) * DH])
+            quantise_and_project(c, (n,), by_scalar[:, part])
+            quantise_and_project(c, (2 + n,), by_vector[:, part])
 
         squares = keep.tile([P, HEADS, DH], BF16)
         sum_sq = keep.tile([P, HEADS], F32)
@@ -148,76 +165,82 @@ def tile_grouplinearblock_pa_k_kernel(tc, x, norm_bias, w_lin, kernel, out):
         out_rows = keep.tile([P, HEADS * F], F32)
 
         def square_sums(pair):
-            for h in pair:
+            for s in range(2 * pair, 2 * pair + 2):
                 nc.scalar.activation(
-                    out=squares[:, h, :], in_=acc[h][:], func=ACT.Square, accum_out=sum_sq[:, h : h + 1]
+                    out=squares[:, s, :],
+                    in_=acc[FINISH_ORDER[s]][:],
+                    func=ACT.Square,
+                    accum_out=sum_sq[:, s : s + 1],
                 )
-            both = slice(pair[0], pair[0] + 2)
+            both = slice(2 * pair, 2 * pair + 2)
             nc.scalar.activation(
                 out=root[:, both], in_=sum_sq[:, both], func=ACT.Sqrt, scale=1.0 / DH, bias=eps[:]
             )
 
         def gains(pair):
-            both = slice(pair[0], pair[0] + 2)
+            both = slice(2 * pair, 2 * pair + 2)
             nc.vector.reciprocal(out=gain[:, both], in_=root[:, both])
 
         turned_u = {}
 
-        def blend(h):
-            mixed = keep.tile([P, PACK, P], F32, name="mixed%d" % h)
+        def blend(s):
+            h = FINISH_ORDER[s]
+            mixed = keep.tile([P, PACK, P], F32, name="mixed%d" % s)
             nc.vector.scalar_tensor_tensor(
                 out=mixed[:],
                 in0=acc[h][:].rearrange("m (p j) -> m j p", j=PACK),
-                scalar=gain[:, h : h + 1],
+                scalar=gain[:, s : s + 1],
                 in1=bias_rows[:, h, :].rearrange("m (p j) -> m j p", j=PACK),
                 op0=ALU.mult,
                 op1=ALU.add,
             )
-            turned_u[h] = work.tile([P, PACK, TOKENS], F32, tag="work", name="turned_u%d" % h)
+            turned_u[s] = work.tile([P, PACK, TOKENS], F32, tag="work", name="turned_u%d" % s)
             for j in range(PACK):
-                nc.tensor.transpose(out=turned_u[h][:, j, :], in_=mixed[:, j, :], identity=ident_f32[:])
+                nc.tensor.transpose(out=turned_u[s][:, j, :], in_=mixed[:, j, :], identity=ident[:])
 
-        def gather(h):
+        def gather(s):
             nc.scalar.mul(
-                out=u_grouped[:, h * K_PASS : (h + 1) * K_PASS].rearrange("p (r j) -> p r j", j=PACK),
-                in_=turned_u[h][:].rearrange("p j r -> p r j"),
+                out=u_grouped[:, s * K_PASS : (s + 1) * K_PASS].rearrange("p (r j) -> p r j", j=PACK),
+                in_=turned_u[s][:].rearrange("p j r -> p r j"),
                 mul=1.0 / math.sqrt(2.0),
             )
 
-        def second_product(pair):
-            lo = pair[0]
+        def quantise_u(pair):
             quantise(
-                u_grouped[:, lo * K_PASS : (lo + 2) * K_PASS],
-                u_codes[:, lo * TOKENS : (lo + 2) * TOKENS],
-                u_scales[:, lo * TOKENS : (lo + 2) * TOKENS],
+                u_grouped[:, 2 * pair * K_PASS : (2 * pair + 2) * K_PASS],
+                u_codes[:, 2 * pair * TOKENS : (2 * pair + 2) * TOKENS],
+                u_scales[:, 2 * pair * TOKENS : (2 * pair + 2) * TOKENS],
             )
-            for h in pair:
-                y = work.tile([P, F], F32, tag="work")
-                nc.tensor.matmul_mx(
-                    out=y[:],
-                    lhsT=u_codes[:, h * TOKENS : (h + 1) * TOKENS].bitcast(FP8X4),
-                    lhsT_scale=u_scales[:, h * TOKENS : (h + 1) * TOKENS],
-                    rhs=k_codes[:, h * F : (h + 1) * F].bitcast(FP8X4),
-                    rhs_scale=k_scales[:, h * F : (h + 1) * F],
-                    start=True,
-                    stop=True,
-                )
-                copy = nc.scalar.copy if h % 2 == 0 else nc.vector.tensor_copy
-                copy(out=out_rows[:, h * F : (h + 1) * F], in_=y[:])
-            nc.sync.dma_start(out=out[:, lo * F : (lo + 2) * F], in_=out_rows[:, lo * F : (lo + 2) * F])
 
-        first, last = (2, 3), (0, 1)
-        square_sums(first)
-        gains(first)
-        square_sums(last)
-        blend(2)
-        blend(3)
-        gains(last)
-        gather(2)
-        gather(3)
+        def second_product(s):
+            h = FINISH_ORDER[s]
+            y = work.tile([P, F], F32, tag="work")
+            nc.tensor.matmul_mx(
+                out=y[:],
+                lhsT=u_codes[:, s * TOKENS : (s + 1) * TOKENS].bitcast(FP8X4),
+                lhsT_scale=u_scales[:, s * TOKENS : (s + 1) * TOKENS],
+                rhs=k_codes[:, h * F : (h + 1) * F].bitcast(FP8X4),
+                rhs_scale=k_scales[:, h * F : (h + 1) * F],
+                start=True,
+                stop=True,
+            )
+            copy = nc.scalar.copy if s % 2 == 0 else nc.vector.tensor_copy
+            copy(out=out_rows[:, h * F : (h + 1) * F], in_=y[:])
+            nc.sync.dma_start(out=out[:, h * F : (h + 1) * F], in_=out_rows[:, h * F : (h + 1) * F])
+
+        square_sums(0)
+        gains(0)
+        square_sums(1)
         blend(0)
         blend(1)
+        gains(1)
         gather(0)
         gather(1)
-        second_product(first)
-        second_product(last)
+        blend(2)
+        blend(3)
+        gather(2)
+        gather(3)
+        quantise_u(0)
+        quantise_u(1)
+        for s in range(HEADS):
+            second_product(s)

@@ -27,6 +27,9 @@ EPSILON = 1e-6
 HALF = WIDTH // 2
 QUANT_IN = HALF * PACK
 RUN = 4
+TURN_COLS = 256
+FIRST_TURN = 2
+SCALAR_COLS = 1120
 RAW_BUFS = 5
 GROUPED_BUFS = 6
 FINISH_ORDER = [0, 2, 1, 3]
@@ -57,6 +60,8 @@ def tile_grouplinearblock_pa_k_kernel(tc, x, norm_bias, w_lin, kernel, out):
 
         ident = keep.tile([P, P], F32)
         masks.make_identity(nc, ident[:])
+        ident_bf16 = keep.tile([P, P], BF16)
+        masks.make_identity(nc, ident_bf16[:])
         eps = keep.tile([P, 1], F32)
         nc.vector.memset(eps[:], EPSILON)
         table_warm = keep.tile([P, 1], F32)
@@ -130,9 +135,25 @@ def tile_grouplinearblock_pa_k_kernel(tc, x, norm_bias, w_lin, kernel, out):
             rows = raw_pool.tile([P, PACK, WIDTH], BF16, tag="raw")
             nc.sync.dma_start(out=rows[:], in_=pass_rows(c))
             by_scalar = grouped_pool.tile([P, QUANT_IN], BF16, tag="grouped", align_bytes=64)
-            regroup(nc.scalar.copy, by_scalar[:], rows[:, :, 0:HALF])
             by_vector = grouped_pool.tile([P, QUANT_IN], BF16, tag="grouped", align_bytes=64)
-            regroup(nc.vector.tensor_copy, by_vector[:], rows[:, :, HALF:WIDTH])
+            turn = TURN_COLS if c >= FIRST_TURN else 0
+            edge = SCALAR_COLS if c >= FIRST_TURN else 1024
+            if edge > HALF:
+                regroup(nc.scalar.copy, by_vector[:, 0 : (edge - HALF) * PACK], rows[:, :, HALF:edge])
+            regroup(nc.scalar.copy, by_scalar[:, turn * PACK : QUANT_IN], rows[:, :, turn:HALF])
+            if turn:
+                turned_w = work.tile([P, TURN_COLS * PACK], BF16, tag="work")
+                for n in range(2):
+                    cols = slice(n * TURN_COLS // 2, (n + 1) * TURN_COLS // 2)
+                    nc.tensor.matmul(
+                        out=turned_w[:, n * DH : (n + 1) * DH],
+                        lhsT=ident_bf16[:],
+                        rhs=rows[:, :, cols].rearrange("p j w -> p w j"),
+                        start=True,
+                        stop=True,
+                    )
+                nc.scalar.copy(out=by_scalar[:, 0 : TURN_COLS * PACK], in_=turned_w[:])
+            regroup(nc.vector.tensor_copy, by_vector[:, (edge - HALF) * PACK : QUANT_IN], rows[:, :, edge:WIDTH])
             if c > 0:
                 quantise_and_project(c - 1, (0, 1), waiting[:])
             quantise_and_project(c, (2, 3), by_vector[:])

@@ -26,13 +26,14 @@ EPSILON = 1e-6
 
 HALF = WIDTH // 2
 QUANT_IN = HALF * PACK
-RUN = 4
 TURN_COLS = 256
-FIRST_TURN = 2
-SCALAR_COLS = 1120
+TURN_PASSES = range(2, 15)
+JOINT = ()
+RUN = 4
 RAW_BUFS = 5
 GROUPED_BUFS = 6
-FINISH_ORDER = [0, 2, 1, 3]
+OPERAND_BUFS = 6
+ORDER = ["X0","X1","K","W0","W1","W2","W3","W4","W5","W6","W7","W8","W9","W10","W11","W12","W13","W14"]
 
 FLOPS = 2 * TOKENS * WI * WIDTH + 2 * TOKENS * DH * F * HEADS
 
@@ -50,7 +51,7 @@ def tile_grouplinearblock_pa_k_kernel(tc, x, norm_bias, w_lin, kernel, out):
         keep = ctx.enter_context(tc.tile_pool(name="keep", bufs=1))
         raw_pool = ctx.enter_context(tc.tile_pool(name="raw", bufs=RAW_BUFS))
         grouped_pool = ctx.enter_context(tc.tile_pool(name="grouped", bufs=GROUPED_BUFS))
-        operand_pool = ctx.enter_context(tc.tile_pool(name="operand", bufs=GROUPED_BUFS))
+        operand_pool = ctx.enter_context(tc.tile_pool(name="operand", bufs=OPERAND_BUFS))
         acc_pool = ctx.enter_context(tc.psum_pool(name="acc", bufs=1))
         work = ctx.enter_context(tc.psum_pool(name="work", bufs=4))
         ctx.enter_context(tc.manual_schedule())
@@ -65,60 +66,76 @@ def tile_grouplinearblock_pa_k_kernel(tc, x, norm_bias, w_lin, kernel, out):
         eps = keep.tile([P, 1], F32)
         nc.vector.memset(eps[:], EPSILON)
         table_warm = keep.tile([P, 1], F32)
-        nc.scalar.activation(out=table_warm[:], in_=eps[:], func=ACT.Sqrt)
-
-        x_rows = raw_pool.tile([P, WI], BF16, tag="raw")
-        x_piece = WI // 4
-        for q in range(4):
-            cols = slice(q * x_piece, (q + 1) * x_piece)
-            nc.sync.dma_start(out=x_rows[:, cols], in_=x[:, cols])
-        k_rows = raw_pool.tile([P, HEADS, PACK, F], BF16, tag="raw")
-        nc.sync.dma_start(out=k_rows[:], in_=kernel.rearrange("h (p j) f -> p h j f", j=PACK))
-
-        x_words = x_rows[:].bitcast(F32).rearrange("m (c p u) -> m c u p", p=P, u=2)
-        x_grouped = [
-            grouped_pool.tile([P, QUANT_IN], BF16, tag="grouped", name="x_grouped%d" % g, align_bytes=64)
-            for g in range(2)
-        ]
-        x_codes = keep.tile([P, PASSES * TOKENS], U32, align_bytes=64)
-        x_scales = keep.tile([P, PASSES * TOKENS], U8, align_bytes=64)
-        for b in range(PASSES // 2):
-            turned = work.tile([P, 2, 2, TOKENS], F32, tag="work")
-            for cc in range(2):
-                for u in range(2):
-                    nc.tensor.transpose(
-                        out=turned[:, cc, u, :], in_=x_words[:, 2 * b + cc, u, :], identity=ident[:]
-                    )
-            words = x_grouped[b // 4][:].bitcast(F32)[:, (b % 4) * 512 : (b % 4 + 1) * 512]
-            copy = nc.scalar.copy if b % 2 == 0 else nc.vector.tensor_copy
-            copy(
-                out=words.rearrange("p (c r u) -> p c r u", c=2, u=2),
-                in_=turned[:].rearrange("p c u r -> p c r u"),
-            )
-        for g in range(2):
-            cols = slice(g * HALF, (g + 1) * HALF)
-            quantise(x_grouped[g][:], x_codes[:, cols], x_scales[:, cols])
-
-        k_grouped = grouped_pool.tile([P, QUANT_IN], BF16, tag="grouped", align_bytes=64)
-        k_codes = keep.tile([P, HEADS * F], U32, align_bytes=64)
-        k_scales = keep.tile([P, HEADS * F], U8, align_bytes=64)
-        for h in range(HEADS):
-            copy = nc.scalar.copy if h % 2 == 0 else nc.vector.tensor_copy
-            regroup(copy, k_grouped[:, h * F * PACK : (h + 1) * F * PACK], k_rows[:, h])
-        quantise(k_grouped[:], k_codes[:], k_scales[:])
+        nc.scalar.activation(out=table_warm[:], in_=eps[:], func=ACT.Abs_reciprocal_sqrt)
 
         acc = [acc_pool.tile([P, DH], F32, name="acc%d" % h) for h in range(HEADS)]
 
-        def quantise_and_project(c, heads, grouped):
-            width = len(heads) * DH
-            codes = operand_pool.tile([P, HALF], U32, tag="codes", align_bytes=64)
-            scales = operand_pool.tile([P, HALF], U8, tag="scales", align_bytes=64)
-            quantise(grouped, codes[:, 0:width], scales[:, 0:width])
+        def pass_rows(c):
+            return w_lin[c * K_PASS : (c + 1) * K_PASS, :].rearrange("(p j) w -> p j w", j=PACK)
+
+        def load_w(c):
+            rows = raw_pool.tile([P, PACK, WIDTH], BF16, tag="raw", name="rows%d" % c)
+            pieces = 2 if c == PASSES - 1 else 2 if c in JOINT else 1
+            for n in range(pieces):
+                cols = slice(n * WIDTH // pieces, (n + 1) * WIDTH // pieces)
+                nc.sync.dma_start(out=rows[:, :, cols], in_=pass_rows(c)[:, :, cols])
+            return rows
+
+        def pass_pieces(c):
+            if c == PASSES - 1:
+                return [(n * DH, n * DH + 256, (n + 1) * DH) for n in range(4)]
+            if c in JOINT:
+                if c in TURN_PASSES:
+                    return [(0, 640, HALF), (HALF, HALF + 480, WIDTH)]
+                return [(0, 512, HALF), (HALF, HALF + 512, WIDTH)]
+            return [(HALF, 1120 if c in TURN_PASSES else 1024, WIDTH), (0, HALF, HALF)]
+
+        banks = {}
+
+        def turn(c, rows):
+            banks[c] = work.tile([P, TURN_COLS * PACK], BF16, tag="work", name="w_turned")
+            for n in range(2):
+                cols = slice(n * TURN_COLS // 2, (n + 1) * TURN_COLS // 2)
+                nc.tensor.matmul(
+                    out=banks[c][:, n * DH : (n + 1) * DH],
+                    lhsT=ident_bf16[:],
+                    rhs=rows[:, :, cols].rearrange("p j w -> p w j"),
+                    start=True,
+                    stop=True,
+                )
+
+        def regroup_piece(c, rows, piece):
+            start, middle, stop = piece
+            grouped = grouped_pool.tile([P, QUANT_IN], BF16, tag="grouped", name="grouped%d_%d" % (c, start), align_bytes=64)
+            turned = TURN_COLS if c in TURN_PASSES and start == 0 else 0
+            if start + turned < middle:
+                regroup(
+                    nc.scalar.copy,
+                    grouped[:, turned * PACK : (middle - start) * PACK],
+                    rows[:, :, start + turned : middle],
+                )
+            if turned:
+                nc.scalar.copy(out=grouped[:, 0 : turned * PACK], in_=banks[c][:])
+            if middle < stop:
+                regroup(
+                    nc.vector.tensor_copy,
+                    grouped[:, (middle - start) * PACK : (stop - start) * PACK],
+                    rows[:, :, middle:stop],
+                )
+            return c, start, stop, grouped
+
+        unmatched = []
+        x_ready = set()
+
+        def project(c, start, codes, scales):
+            if c // 8 not in x_ready:
+                unmatched.append((c, start, codes, scales))
+                return
             tokens = slice(c * TOKENS, (c + 1) * TOKENS)
-            for n, h in enumerate(heads):
+            for n in range(codes.shape[1] // DH):
                 cols = slice(n * DH, (n + 1) * DH)
                 nc.tensor.matmul_mx(
-                    out=acc[h][:],
+                    out=acc[start // DH + n][:],
                     lhsT=x_codes[:, tokens].bitcast(FP8X4),
                     lhsT_scale=x_scales[:, tokens],
                     rhs=codes[:, cols].bitcast(FP8X4),
@@ -127,141 +144,202 @@ def tile_grouplinearblock_pa_k_kernel(tc, x, norm_bias, w_lin, kernel, out):
                     stop=(c == PASSES - 1),
                 )
 
-        def pass_rows(c):
-            return w_lin[c * K_PASS : (c + 1) * K_PASS, :].rearrange("(p j) w -> p j w", j=PACK)
+        def quantise_and_project(c, start, stop, grouped):
+            width = stop - start
+            codes = operand_pool.tile([P, HALF], U32, tag="codes", align_bytes=64)
+            scales = operand_pool.tile([P, HALF], U8, tag="scales", align_bytes=64)
+            quantise(grouped[:, 0 : width * PACK], codes[:, 0:width], scales[:, 0:width])
+            project(c, start, codes[:, 0:width], scales[:, 0:width])
 
-        waiting = None
-        for c in range(PASSES - 1):
-            rows = raw_pool.tile([P, PACK, WIDTH], BF16, tag="raw")
-            nc.sync.dma_start(out=rows[:], in_=pass_rows(c))
-            by_scalar = grouped_pool.tile([P, QUANT_IN], BF16, tag="grouped", align_bytes=64)
-            by_vector = grouped_pool.tile([P, QUANT_IN], BF16, tag="grouped", align_bytes=64)
-            turn = TURN_COLS if c >= FIRST_TURN else 0
-            edge = SCALAR_COLS if c >= FIRST_TURN else 1024
-            if edge > HALF:
-                regroup(nc.scalar.copy, by_vector[:, 0 : (edge - HALF) * PACK], rows[:, :, HALF:edge])
-            regroup(nc.scalar.copy, by_scalar[:, turn * PACK : QUANT_IN], rows[:, :, turn:HALF])
-            if turn:
-                turned_w = work.tile([P, TURN_COLS * PACK], BF16, tag="work")
-                for n in range(2):
-                    cols = slice(n * TURN_COLS // 2, (n + 1) * TURN_COLS // 2)
-                    nc.tensor.matmul(
-                        out=turned_w[:, n * DH : (n + 1) * DH],
-                        lhsT=ident_bf16[:],
-                        rhs=rows[:, :, cols].rearrange("p j w -> p w j"),
-                        start=True,
-                        stop=True,
-                    )
-                nc.scalar.copy(out=by_scalar[:, 0 : TURN_COLS * PACK], in_=turned_w[:])
-            regroup(nc.vector.tensor_copy, by_vector[:, (edge - HALF) * PACK : QUANT_IN], rows[:, :, edge:WIDTH])
-            if c > 0:
-                quantise_and_project(c - 1, (0, 1), waiting[:])
-            quantise_and_project(c, (2, 3), by_vector[:])
-            waiting = by_scalar
+        x_rows = keep.tile([P, WI], BF16)
+        x_words = x_rows[:].bitcast(F32).rearrange("m (c p u) -> m c u p", p=P, u=2)
+        x_codes = keep.tile([P, PASSES * TOKENS], U32, align_bytes=64)
+        x_scales = keep.tile([P, PASSES * TOKENS], U8, align_bytes=64)
+        k_rows = keep.tile([P, HEADS, PACK, F], BF16)
+        k_hbm = kernel.rearrange("h (p j) f -> p h j f", j=PACK)
+        k_codes = keep.tile([P, HEADS * F], U32, align_bytes=64)
+        k_scales = keep.tile([P, HEADS * F], U8, align_bytes=64)
+        loaded = {}
+        for name in ORDER:
+            n = int(name[1:]) if len(name) > 1 else 0
+            if name[0] == "X":
+                step = WI // 2 // 2
+                for i in range(2):
+                    cols = slice(n * WI // 2 + i * step, n * WI // 2 + (i + 1) * step)
+                    nc.sync.dma_start(out=x_rows[:, cols], in_=x[:, cols])
+            elif name[0] == "K":
+                step = HEADS // 1
+                for i in range(0, HEADS, step):
+                    nc.sync.dma_start(out=k_rows[:, i : i + step], in_=k_hbm[:, i : i + step])
+            else:
+                loaded[n] = load_w(n)
+        waiting = []
+
+        def flush():
+            todo = list(waiting)
+            waiting.clear()
+            for step in todo:
+                step()
+
+        def later(f):
+            flush()
+            waiting.append(f)
+
+        def do_x(g):
+            grouped = grouped_pool.tile([P, QUANT_IN], BF16, tag="grouped", name="x_grouped%d" % g, align_bytes=64)
+            for b in range(4):
+                turned = work.tile([P, 2, 2, TOKENS], F32, tag="work", name="x_turned")
+                for cc in range(2):
+                    for u in range(2):
+                        nc.tensor.transpose(
+                            out=turned[:, cc, u, :], in_=x_words[:, 8 * g + 2 * b + cc, u, :], identity=ident[:]
+                        )
+                words = grouped[:].bitcast(F32)[:, b * 512 : (b + 1) * 512]
+                copy = nc.vector.tensor_copy if b in (1, 3) else nc.scalar.copy
+                copy(
+                    out=words.rearrange("p (c r u) -> p c r u", c=2, u=2),
+                    in_=turned[:].rearrange("p c u r -> p c r u"),
+                )
+
+            def finish():
+                cols = slice(g * HALF, (g + 1) * HALF)
+                quantise(grouped[:], x_codes[:, cols], x_scales[:, cols])
+                x_ready.add(g)
+                todo = list(unmatched)
+                unmatched.clear()
+                for t in todo:
+                    project(*t)
+
+            later(finish)
+
+        def do_k():
+            grouped = grouped_pool.tile([P, QUANT_IN], BF16, tag="grouped", name="k_grouped", align_bytes=64)
+            for h in range(HEADS):
+                copy = nc.vector.tensor_copy if h in (1, 3) else nc.scalar.copy
+                regroup(copy, grouped[:, h * F * PACK : (h + 1) * F * PACK], k_rows[:, h])
+            later(lambda: quantise(grouped[:], k_codes[:], k_scales[:]))
+
+        def do_w(c):
+            if c in TURN_PASSES:
+                turn(c, loaded[c])
+            for piece in pass_pieces(c):
+                r = regroup_piece(c, loaded[c], piece)
+                later(lambda r=r: quantise_and_project(*r))
+
+        for name in ORDER:
+            if name[0] == "X":
+                do_x(int(name[1:]))
+            elif name[0] == "K":
+                do_k()
+            else:
+                do_w(int(name[1:]))
 
         c = PASSES - 1
-        rows = raw_pool.tile([P, PACK, WIDTH], BF16, tag="raw")
-        for h in FINISH_ORDER:
-            cols = slice(h * DH, (h + 1) * DH)
-            nc.sync.dma_start(out=rows[:, :, cols], in_=pass_rows(c)[:, :, cols])
+        rows = load_w(c)
         bias_rows = keep.tile([P, HEADS, DH], BF16)
         nc.sync.dma_start(out=bias_rows[:], in_=norm_bias)
-        quantise_and_project(c - 1, (0, 1), waiting[:])
-        by_scalar = grouped_pool.tile([P, QUANT_IN], BF16, tag="grouped", align_bytes=64)
-        by_vector = grouped_pool.tile([P, QUANT_IN], BF16, tag="grouped", align_bytes=64)
-        for n in range(2):
-            part = slice(n * DH * PACK, (n + 1) * DH * PACK)
-            regroup(nc.scalar.copy, by_scalar[:, part], rows[:, :, n * DH : (n + 1) * DH])
-            regroup(nc.vector.tensor_copy, by_vector[:, part], rows[:, :, HALF + n * DH : HALF + (n + 1) * DH])
-            quantise_and_project(c, (n,), by_scalar[:, part])
-            quantise_and_project(c, (2 + n,), by_vector[:, part])
-
         squares = keep.tile([P, HEADS, DH], BF16)
-        sum_sq = keep.tile([P, HEADS], F32)
-        root = keep.tile([P, HEADS], F32)
-        gain = keep.tile([P, HEADS], F32)
+        sum_sq = [keep.tile([P, 1], F32, name="sum_sq%d" % h) for h in range(HEADS)]
+        gain = [keep.tile([P, 1], F32, name="gain%d" % h) for h in range(HEADS)]
         u_grouped = keep.tile([P, HEADS * TOKENS * PACK], BF16, align_bytes=64)
         u_codes = keep.tile([P, HEADS * TOKENS], U32, align_bytes=64)
         u_scales = keep.tile([P, HEADS * TOKENS], U8, align_bytes=64)
         out_rows = keep.tile([P, HEADS * F], F32)
 
-        def square_sums(pair):
-            for s in range(2 * pair, 2 * pair + 2):
-                nc.scalar.activation(
-                    out=squares[:, s, :],
-                    in_=acc[FINISH_ORDER[s]][:],
-                    func=ACT.Square,
-                    accum_out=sum_sq[:, s : s + 1],
-                )
-            both = slice(2 * pair, 2 * pair + 2)
-            nc.scalar.activation(
-                out=root[:, both], in_=sum_sq[:, both], func=ACT.Sqrt, scale=1.0 / DH, bias=eps[:]
-            )
+        def norm(h):
+            nc.scalar.activation(out=squares[:, h, :], in_=acc[h][:], func=ACT.Square, accum_out=sum_sq[h][:])
 
-        def gains(pair):
-            both = slice(2 * pair, 2 * pair + 2)
-            nc.vector.reciprocal(out=gain[:, both], in_=root[:, both])
+        def root(h):
+            nc.scalar.activation(
+                out=gain[h][:], in_=sum_sq[h][:], func=ACT.Abs_reciprocal_sqrt, scale=1.0 / DH, bias=eps[:]
+            )
 
         turned_u = {}
 
-        def blend(s):
-            h = FINISH_ORDER[s]
-            mixed = keep.tile([P, PACK, P], F32, name="mixed%d" % s)
+        def blend(h):
+            mixed = keep.tile([P, PACK, P], F32, name="mixed%d" % h)
             nc.vector.scalar_tensor_tensor(
                 out=mixed[:],
                 in0=acc[h][:].rearrange("m (p j) -> m j p", j=PACK),
-                scalar=gain[:, s : s + 1],
+                scalar=gain[h][:],
                 in1=bias_rows[:, h, :].rearrange("m (p j) -> m j p", j=PACK),
                 op0=ALU.mult,
                 op1=ALU.add,
             )
-            turned_u[s] = work.tile([P, PACK, TOKENS], F32, tag="work", name="turned_u%d" % s)
+            turned_u[h] = work.tile([P, PACK, TOKENS], F32, tag="work", name="turned_u%d" % h)
             for j in range(PACK):
-                nc.tensor.transpose(out=turned_u[s][:, j, :], in_=mixed[:, j, :], identity=ident[:])
+                nc.tensor.transpose(out=turned_u[h][:, j, :], in_=mixed[:, j, :], identity=ident[:])
 
-        def gather(s):
+        def gather(h):
             nc.scalar.mul(
-                out=u_grouped[:, s * K_PASS : (s + 1) * K_PASS].rearrange("p (r j) -> p r j", j=PACK),
-                in_=turned_u[s][:].rearrange("p j r -> p r j"),
+                out=u_grouped[:, h * K_PASS : (h + 1) * K_PASS].rearrange("p (r j) -> p r j", j=PACK),
+                in_=turned_u[h][:].rearrange("p j r -> p r j"),
                 mul=1.0 / math.sqrt(2.0),
             )
 
-        def quantise_u(pair):
-            quantise(
-                u_grouped[:, 2 * pair * K_PASS : (2 * pair + 2) * K_PASS],
-                u_codes[:, 2 * pair * TOKENS : (2 * pair + 2) * TOKENS],
-                u_scales[:, 2 * pair * TOKENS : (2 * pair + 2) * TOKENS],
+        def gather_by_vector(h):
+            nc.vector.tensor_scalar(
+                out=u_grouped[:, h * K_PASS : (h + 1) * K_PASS].rearrange("p (r j) -> p r j", j=PACK),
+                in0=turned_u[h][:].rearrange("p j r -> p r j"),
+                scalar1=1.0 / math.sqrt(2.0),
+                scalar2=None,
+                op0=ALU.mult,
             )
 
-        def second_product(s):
-            h = FINISH_ORDER[s]
-            y = work.tile([P, F], F32, tag="work")
+        y = {}
+
+        def second_product(h):
+            tokens = slice(h * TOKENS, (h + 1) * TOKENS)
+            quantise(u_grouped[:, h * K_PASS : (h + 1) * K_PASS], u_codes[:, tokens], u_scales[:, tokens])
+            y[h] = work.tile([P, F], F32, tag="work", name="y%d" % h)
             nc.tensor.matmul_mx(
-                out=y[:],
-                lhsT=u_codes[:, s * TOKENS : (s + 1) * TOKENS].bitcast(FP8X4),
-                lhsT_scale=u_scales[:, s * TOKENS : (s + 1) * TOKENS],
+                out=y[h][:],
+                lhsT=u_codes[:, tokens].bitcast(FP8X4),
+                lhsT_scale=u_scales[:, tokens],
                 rhs=k_codes[:, h * F : (h + 1) * F].bitcast(FP8X4),
                 rhs_scale=k_scales[:, h * F : (h + 1) * F],
                 start=True,
                 stop=True,
             )
-            copy = nc.scalar.copy if s % 2 == 0 else nc.vector.tensor_copy
-            copy(out=out_rows[:, h * F : (h + 1) * F], in_=y[:])
+
+        def store(h, copy):
+            copy(out=out_rows[:, h * F : (h + 1) * F], in_=y[h][:])
             nc.sync.dma_start(out=out[:, h * F : (h + 1) * F], in_=out_rows[:, h * F : (h + 1) * F])
 
-        square_sums(0)
-        gains(0)
-        square_sums(1)
+        if c in TURN_PASSES:
+            turn(c, rows)
+        parts = [None] * HEADS
+        pieces = pass_pieces(c)
+        parts[0] = regroup_piece(c, rows, pieces[0])
+        flush()
+        parts[1] = regroup_piece(c, rows, pieces[1])
+        quantise_and_project(*parts[0])
+        parts[2] = regroup_piece(c, rows, pieces[2])
+        quantise_and_project(*parts[1])
+        parts[3] = regroup_piece(c, rows, pieces[3])
+        quantise_and_project(*parts[2])
+        quantise_and_project(*parts[3])
+        norm(0)
+        root(0)
+        norm(1)
+        root(1)
+        norm(2)
+        root(2)
+        norm(3)
+        root(3)
         blend(0)
         blend(1)
-        gains(1)
-        gather(0)
-        gather(1)
         blend(2)
         blend(3)
+        gather(0)
+        gather(1)
+        second_product(0)
         gather(2)
+        second_product(1)
         gather(3)
-        quantise_u(0)
-        quantise_u(1)
-        for s in range(HEADS):
-            second_product(s)
+        store(0, nc.vector.tensor_copy)
+        second_product(2)
+        store(1, nc.vector.tensor_copy)
+        second_product(3)
+        store(2, nc.scalar.copy)
+        store(3, nc.vector.tensor_copy)

@@ -29,7 +29,9 @@ QUANT_IN = HALF * PACK
 TURN_COLS = 256
 TURN_PASSES = range(2, 15)
 JOINT = ()
-RUN = 4
+SCALAR_RUN = 8
+KV = (1, 3)
+VECTOR_RUN = 4
 RAW_BUFS = 5
 GROUPED_BUFS = 6
 OPERAND_BUFS = 6
@@ -38,10 +40,10 @@ ORDER = ["X0","X1","K","W0","W1","W2","W3","W4","W5","W6","W7","W8","W9","W10","
 FLOPS = 2 * TOKENS * WI * WIDTH + 2 * TOKENS * DH * F * HEADS
 
 
-def regroup(copy, grouped, rows):
+def regroup(copy, grouped, rows, run):
     copy(
-        out=grouped.rearrange("p (c i j) -> p c j i", i=RUN, j=PACK),
-        in_=rows.rearrange("p j (c i) -> p c j i", i=RUN),
+        out=grouped.rearrange("p (c i j) -> p c j i", i=run, j=PACK),
+        in_=rows.rearrange("p j (c i) -> p c j i", i=run),
     )
 
 
@@ -113,6 +115,7 @@ def tile_grouplinearblock_pa_k_kernel(tc, x, norm_bias, w_lin, kernel, out):
                     nc.scalar.copy,
                     grouped[:, turned * PACK : (middle - start) * PACK],
                     rows[:, :, start + turned : middle],
+                    SCALAR_RUN,
                 )
             if turned:
                 nc.scalar.copy(out=grouped[:, 0 : turned * PACK], in_=banks[c][:])
@@ -121,6 +124,7 @@ def tile_grouplinearblock_pa_k_kernel(tc, x, norm_bias, w_lin, kernel, out):
                     nc.vector.tensor_copy,
                     grouped[:, (middle - start) * PACK : (stop - start) * PACK],
                     rows[:, :, middle:stop],
+                    VECTOR_RUN,
                 )
             return c, start, stop, grouped
 
@@ -215,8 +219,8 @@ def tile_grouplinearblock_pa_k_kernel(tc, x, norm_bias, w_lin, kernel, out):
         def do_k():
             grouped = grouped_pool.tile([P, QUANT_IN], BF16, tag="grouped", name="k_grouped", align_bytes=64)
             for h in range(HEADS):
-                copy = nc.vector.tensor_copy if h in (1, 3) else nc.scalar.copy
-                regroup(copy, grouped[:, h * F * PACK : (h + 1) * F * PACK], k_rows[:, h])
+                copy = nc.vector.tensor_copy if h in KV else nc.scalar.copy
+                regroup(copy, grouped[:, h * F * PACK : (h + 1) * F * PACK], k_rows[:, h], VECTOR_RUN if h in KV else SCALAR_RUN)
             later(lambda: quantise(grouped[:], k_codes[:], k_scales[:]))
 
         def do_w(c):

from contextlib import ExitStack
import math

import concourse.masks as masks
import concourse.mybir as mybir

BF16 = mybir.dt.bfloat16
F32 = mybir.dt.float32
U32 = mybir.dt.uint32
U8 = mybir.dt.uint8
FP8X4 = mybir.dt.float8_e4m3fn_x4
ACT = mybir.ActivationFunctionType
ALU = mybir.AluOpType

P = 128
PACK = 4
K_PASS = P * PACK
TOKENS = 128
WI = 8192
HEADS = 4
DH = 512
F = 256
WIDTH = HEADS * DH
PASSES = WI // K_PASS
EPSILON = 1e-6

HALF = WIDTH // 2
QUANT_IN = HALF * PACK
TURN_COLS = 256
TURN_PASSES = range(2, 15)
JOINT = ()
SCALAR_RUN = 8
KV = (1, 3)
VECTOR_RUN = 4
RAW_BUFS = 5
GROUPED_BUFS = 6
OPERAND_BUFS = 6
ORDER = ["X0","X1","K","W0","W1","W2","W3","W4","W5","W6","W7","W8","W9","W10","W11","W12","W13","W14"]

FLOPS = 2 * TOKENS * WI * WIDTH + 2 * TOKENS * DH * F * HEADS


def regroup(copy, grouped, rows, run):
    copy(
        out=grouped.rearrange("p (c i j) -> p c j i", i=run, j=PACK),
        in_=rows.rearrange("p j (c i) -> p c j i", i=run),
    )


def tile_grouplinearblock_pa_k_kernel(tc, x, norm_bias, w_lin, kernel, out):
    nc = tc.nc
    with ExitStack() as ctx:
        keep = ctx.enter_context(tc.tile_pool(name="keep", bufs=1))
        raw_pool = ctx.enter_context(tc.tile_pool(name="raw", bufs=RAW_BUFS))
        grouped_pool = ctx.enter_context(tc.tile_pool(name="grouped", bufs=GROUPED_BUFS))
        operand_pool = ctx.enter_context(tc.tile_pool(name="operand", bufs=OPERAND_BUFS))
        acc_pool = ctx.enter_context(tc.psum_pool(name="acc", bufs=1))
        work = ctx.enter_context(tc.psum_pool(name="work", bufs=4))
        ctx.enter_context(tc.manual_schedule())

        def quantise(grouped, codes, scales):
            nc.vector.quantize_mx(out=codes.bitcast(FP8X4), scales=scales, in_=grouped)

        ident = keep.tile([P, P], F32)
        masks.make_identity(nc, ident[:])
        ident_bf16 = keep.tile([P, P], BF16)
        masks.make_identity(nc, ident_bf16[:])
        eps = keep.tile([P, 1], F32)
        nc.vector.memset(eps[:], EPSILON)
        table_warm = keep.tile([P, 1], F32)
        nc.scalar.activation(out=table_warm[:], in_=eps[:], func=ACT.Abs_reciprocal_sqrt)

        acc = [acc_pool.tile([P, DH], F32, name="acc%d" % h) for h in range(HEADS)]

        def pass_rows(c):
            return w_lin[c * K_PASS : (c + 1) * K_PASS, :].rearrange("(p j) w -> p j w", j=PACK)

        def load_w(c):
            rows = raw_pool.tile([P, PACK, WIDTH], BF16, tag="raw", name="rows%d" % c)
            pieces = 2 if c == PASSES - 1 else 2 if c in JOINT else 1
            for n in range(pieces):
                cols = slice(n * WIDTH // pieces, (n + 1) * WIDTH // pieces)
                nc.sync.dma_start(out=rows[:, :, cols], in_=pass_rows(c)[:, :, cols])
            return rows

        def pass_pieces(c):
            if c == PASSES - 1:
                return [(n * DH, n * DH + 256, (n + 1) * DH) for n in range(4)]
            if c in JOINT:
                if c in TURN_PASSES:
                    return [(0, 640, HALF), (HALF, HALF + 480, WIDTH)]
                return [(0, 512, HALF), (HALF, HALF + 512, WIDTH)]
            return [(HALF, 1120 if c in TURN_PASSES else 1024, WIDTH), (0, HALF, HALF)]

        banks = {}

        def turn(c, rows):
            banks[c] = work.tile([P, TURN_COLS * PACK], BF16, tag="work", name="w_turned")
            for n in range(2):
                cols = slice(n * TURN_COLS // 2, (n + 1) * TURN_COLS // 2)
                nc.tensor.matmul(
                    out=banks[c][:, n * DH : (n + 1) * DH],
                    lhsT=ident_bf16[:],
                    rhs=rows[:, :, cols].rearrange("p j w -> p w j"),
                    start=True,
                    stop=True,
                )

        def regroup_piece(c, rows, piece):
            start, middle, stop = piece
            grouped = grouped_pool.tile([P, QUANT_IN], BF16, tag="grouped", name="grouped%d_%d" % (c, start), align_bytes=64)
            turned = TURN_COLS if c in TURN_PASSES and start == 0 else 0
            if start + turned < middle:
                regroup(
                    nc.scalar.copy,
                    grouped[:, turned * PACK : (middle - start) * PACK],
                    rows[:, :, start + turned : middle],
                    SCALAR_RUN,
                )
            if turned:
                nc.scalar.copy(out=grouped[:, 0 : turned * PACK], in_=banks[c][:])
            if middle < stop:
                regroup(
                    nc.vector.tensor_copy,
                    grouped[:, (middle - start) * PACK : (stop - start) * PACK],
                    rows[:, :, middle:stop],
                    VECTOR_RUN,
                )
            return c, start, stop, grouped

        unmatched = []
        x_ready = set()

        def project(c, start, codes, scales):
            if c // 8 not in x_ready:
                unmatched.append((c, start, codes, scales))
                return
            tokens = slice(c * TOKENS, (c + 1) * TOKENS)
            for n in range(codes.shape[1] // DH):
                cols = slice(n * DH, (n + 1) * DH)
                nc.tensor.matmul_mx(
                    out=acc[start // DH + n][:],
                    lhsT=x_codes[:, tokens].bitcast(FP8X4),
                    lhsT_scale=x_scales[:, tokens],
                    rhs=codes[:, cols].bitcast(FP8X4),
                    rhs_scale=scales[:, cols],
                    start=(c == 0),
                    stop=(c == PASSES - 1),
                )

        def quantise_and_project(c, start, stop, grouped):
            width = stop - start
            codes = operand_pool.tile([P, HALF], U32, tag="codes", align_bytes=64)
            scales = operand_pool.tile([P, HALF], U8, tag="scales", align_bytes=64)
            quantise(grouped[:, 0 : width * PACK], codes[:, 0:width], scales[:, 0:width])
            project(c, start, codes[:, 0:width], scales[:, 0:width])

        x_rows = keep.tile([P, WI], BF16)
        x_words = x_rows[:].bitcast(F32).rearrange("m (c p u) -> m c u p", p=P, u=2)
        x_codes = keep.tile([P, PASSES * TOKENS], U32, align_bytes=64)
        x_scales = keep.tile([P, PASSES * TOKENS], U8, align_bytes=64)
        k_rows = keep.tile([P, HEADS, PACK, F], BF16)
        k_hbm = kernel.rearrange("h (p j) f -> p h j f", j=PACK)
        k_codes = keep.tile([P, HEADS * F], U32, align_bytes=64)
        k_scales = keep.tile([P, HEADS * F], U8, align_bytes=64)
        loaded = {}
        for name in ORDER:
            n = int(name[1:]) if len(name) > 1 else 0
            if name[0] == "X":
                step = WI // 2 // 2
                for i in range(2):
                    cols = slice(n * WI // 2 + i * step, n * WI // 2 + (i + 1) * step)
                    nc.sync.dma_start(out=x_rows[:, cols], in_=x[:, cols])
            elif name[0] == "K":
                step = HEADS // 1
                for i in range(0, HEADS, step):
                    nc.sync.dma_start(out=k_rows[:, i : i + step], in_=k_hbm[:, i : i + step])
            else:
                loaded[n] = load_w(n)
        waiting = []

        def flush():
            todo = list(waiting)
            waiting.clear()
            for step in todo:
                step()

        def later(f):
            flush()
            waiting.append(f)

        def do_x(g):
            grouped = grouped_pool.tile([P, QUANT_IN], BF16, tag="grouped", name="x_grouped%d" % g, align_bytes=64)
            for b in range(4):
                turned = work.tile([P, 2, 2, TOKENS], F32, tag="work", name="x_turned")
                for cc in range(2):
                    for u in range(2):
                        nc.tensor.transpose(
                            out=turned[:, cc, u, :], in_=x_words[:, 8 * g + 2 * b + cc, u, :], identity=ident[:]
                        )
                words = grouped[:].bitcast(F32)[:, b * 512 : (b + 1) * 512]
                copy = nc.vector.tensor_copy if b in (1, 3) else nc.scalar.copy
                copy(
                    out=words.rearrange("p (c r u) -> p c r u", c=2, u=2),
                    in_=turned[:].rearrange("p c u r -> p c r u"),
                )

            def finish():
                cols = slice(g * HALF, (g + 1) * HALF)
                quantise(grouped[:], x_codes[:, cols], x_scales[:, cols])
                x_ready.add(g)
                todo = list(unmatched)
                unmatched.clear()
                for t in todo:
                    project(*t)

            later(finish)

        def do_k():
            grouped = grouped_pool.tile([P, QUANT_IN], BF16, tag="grouped", name="k_grouped", align_bytes=64)
            for h in range(HEADS):
                copy = nc.vector.tensor_copy if h in KV else nc.scalar.copy
                regroup(copy, grouped[:, h * F * PACK : (h + 1) * F * PACK], k_rows[:, h], VECTOR_RUN if h in KV else SCALAR_RUN)
            later(lambda: quantise(grouped[:], k_codes[:], k_scales[:]))

        def do_w(c):
            if c in TURN_PASSES:
                turn(c, loaded[c])
            for piece in pass_pieces(c):
                r = regroup_piece(c, loaded[c], piece)
                later(lambda r=r: quantise_and_project(*r))

        for name in ORDER:
            if name[0] == "X":
                do_x(int(name[1:]))
            elif name[0] == "K":
                do_k()
            else:
                do_w(int(name[1:]))

        c = PASSES - 1
        rows = load_w(c)
        bias_rows = keep.tile([P, HEADS, DH], BF16)
        nc.sync.dma_start(out=bias_rows[:], in_=norm_bias)
        squares = keep.tile([P, HEADS, DH], BF16)
        sum_sq = [keep.tile([P, 1], F32, name="sum_sq%d" % h) for h in range(HEADS)]
        gain = [keep.tile([P, 1], F32, name="gain%d" % h) for h in range(HEADS)]
        u_grouped = keep.tile([P, HEADS * TOKENS * PACK], BF16, align_bytes=64)
        u_codes = keep.tile([P, HEADS * TOKENS], U32, align_bytes=64)
        u_scales = keep.tile([P, HEADS * TOKENS], U8, align_bytes=64)
        out_rows = keep.tile([P, HEADS * F], F32)

        def norm(h):
            nc.scalar.activation(out=squares[:, h, :], in_=acc[h][:], func=ACT.Square, accum_out=sum_sq[h][:])

        def root(h):
            nc.scalar.activation(
                out=gain[h][:], in_=sum_sq[h][:], func=ACT.Abs_reciprocal_sqrt, scale=1.0 / DH, bias=eps[:]
            )

        turned_u = {}

        def blend(h):
            mixed = keep.tile([P, PACK, P], F32, name="mixed%d" % h)
            nc.vector.scalar_tensor_tensor(
                out=mixed[:],
                in0=acc[h][:].rearrange("m (p j) -> m j p", j=PACK),
                scalar=gain[h][:],
                in1=bias_rows[:, h, :].rearrange("m (p j) -> m j p", j=PACK),
                op0=ALU.mult,
                op1=ALU.add,
            )
            turned_u[h] = work.tile([P, PACK, TOKENS], F32, tag="work", name="turned_u%d" % h)
            for j in range(PACK):
                nc.tensor.transpose(out=turned_u[h][:, j, :], in_=mixed[:, j, :], identity=ident[:])

        def gather(h):
            nc.scalar.mul(
                out=u_grouped[:, h * K_PASS : (h + 1) * K_PASS].rearrange("p (r j) -> p r j", j=PACK),
                in_=turned_u[h][:].rearrange("p j r -> p r j"),
                mul=1.0 / math.sqrt(2.0),
            )

        def gather_by_vector(h):
            nc.vector.tensor_scalar(
                out=u_grouped[:, h * K_PASS : (h + 1) * K_PASS].rearrange("p (r j) -> p r j", j=PACK),
                in0=turned_u[h][:].rearrange("p j r -> p r j"),
                scalar1=1.0 / math.sqrt(2.0),
                scalar2=None,
                op0=ALU.mult,
            )

        y = {}

        def second_product(h):
            tokens = slice(h * TOKENS, (h + 1) * TOKENS)
            quantise(u_grouped[:, h * K_PASS : (h + 1) * K_PASS], u_codes[:, tokens], u_scales[:, tokens])
            y[h] = work.tile([P, F], F32, tag="work", name="y%d" % h)
            nc.tensor.matmul_mx(
                out=y[h][:],
                lhsT=u_codes[:, tokens].bitcast(FP8X4),
                lhsT_scale=u_scales[:, tokens],
                rhs=k_codes[:, h * F : (h + 1) * F].bitcast(FP8X4),
                rhs_scale=k_scales[:, h * F : (h + 1) * F],
                start=True,
                stop=True,
            )

        def store(h, copy):
            copy(out=out_rows[:, h * F : (h + 1) * F], in_=y[h][:])
            nc.sync.dma_start(out=out[:, h * F : (h + 1) * F], in_=out_rows[:, h * F : (h + 1) * F])

        if c in TURN_PASSES:
            turn(c, rows)
        parts = [None] * HEADS
        pieces = pass_pieces(c)
        parts[0] = regroup_piece(c, rows, pieces[0])
        flush()
        parts[1] = regroup_piece(c, rows, pieces[1])
        quantise_and_project(*parts[0])
        parts[2] = regroup_piece(c, rows, pieces[2])
        quantise_and_project(*parts[1])
        parts[3] = regroup_piece(c, rows, pieces[3])
        quantise_and_project(*parts[2])
        quantise_and_project(*parts[3])
        norm(0)
        root(0)
        norm(1)
        root(1)
        norm(2)
        root(2)
        norm(3)
        root(3)
        blend(0)
        blend(1)
        blend(2)
        blend(3)
        gather(0)
        gather(1)
        second_product(0)
        gather(2)
        second_product(1)
        gather(3)
        store(0, nc.vector.tensor_copy)
        second_product(2)
        store(1, nc.vector.tensor_copy)
        second_product(3)
        store(2, nc.scalar.copy)
        store(3, nc.vector.tensor_copy)
